import numpy as np
import ml_dtypes


def mxq(x, axis, fmt="e4m3"):
    dtype, down = {"e4m3": (ml_dtypes.float8_e4m3fn, 7), "e5m2": (ml_dtypes.float8_e5m2, 14)}[fmt]
    v = np.moveaxis(np.asarray(x, np.float32).astype(ml_dtypes.bfloat16).astype(np.float64), axis, -1)
    blocks = v.reshape(v.shape[:-1] + (-1, 32))
    amax = np.abs(blocks).max(-1, keepdims=True)
    byte = np.maximum(np.where(amax > 0, np.frexp(amax)[1] - 1 + 127, 0) - down, 1)
    scale = np.exp2(byte - 127.0)
    codes = (blocks / scale).astype(np.float32).astype(dtype).astype(np.float64)
    return np.moveaxis((codes * scale).reshape(v.shape), -1, axis)


WIDE = False


def mx_kscale(k):
    if not WIDE:
        return np.ones(k)
    levels = np.array([10, -10, 5, -5, 0])
    if k % 512:
        return np.exp2(np.random.permutation(np.resize(levels, k // 32))).repeat(32)
    a = np.empty((k // 512, 16))
    for p in range(k // 512):
        a[p, :8] = np.random.permutation(np.resize(levels, 8))
        for g in range(8):
            far = levels[np.abs(levels - a[p, g]) >= 10]
            a[p, g + 8] = far[np.random.randint(len(far))]
    return np.exp2(a.ravel()).repeat(32)


BF16 = ml_dtypes.bfloat16


def bf(x):
    return np.asarray(x, np.float32).astype(BF16)


def f64(x):
    return np.asarray(x).astype(np.float64)


B, IN, H, Z, G = 512, 1024, 1024, 256, 4


def setup_inputs():
    s = mx_kscale(IN)
    return {"src_x": bf(np.random.standard_normal((B, IN)) * s),
            "zx": bf(np.random.standard_normal((B, G, Z))),
            "dx_w": bf(np.random.standard_normal((G, H, Z)) / np.sqrt(Z)),
            "w_x": bf(np.random.standard_normal((G, H, IN)) / np.sqrt(IN) / s)}


def core(src_x, zx, dx_w, w_x):
    d_x = (f64(zx).transpose(1, 0, 2) @ f64(dx_w).transpose(0, 2, 1)).transpose(1, 0, 2)
    wx = (mxq(f64(src_x), 1, "e4m3") @ mxq(f64(w_x).reshape(G * H, IN), 1, "e4m3").T).reshape(B, G, H)
    return d_x * wx


def e4m3fn_bytes(y):
    return np.clip(np.asarray(y, np.float64), -448.0, 448.0).astype(np.float32).astype(ml_dtypes.float8_e4m3fn).view(np.uint8)


def reference(src_x, zx, dx_w, w_x):
    out = core(src_x, zx, dx_w, w_x)
    s = np.max(np.abs(out), axis=-1, keepdims=True) / 448.0
    return out, e4m3fn_bytes(out / s)

@@ -1,0 +1,337 @@
+from contextlib import ExitStack
+
+import concourse.mybir as mybir
+from concourse.masks import make_identity
+
+B, IN, H, Z, G = 512, 1024, 1024, 256, 4
+FLOPS = 2 * B * G * H * IN + 2 * B * G * H * Z
+
+F32 = mybir.dt.float32
+BF16 = mybir.dt.bfloat16
+U32 = mybir.dt.uint32
+U8 = mybir.dt.uint8
+FP8X4 = mybir.dt.float8_e4m3fn_x4
+FP8 = mybir.dt.float8_e4m3fn
+ALU = mybir.AluOpType
+ACT = mybir.ActivationFunctionType
+AX = mybir.AxisListType
+
+P = 128
+K_PASS = 4 * P
+PASSES = IN // K_PASS
+WORDS = K_PASS // 2
+CHUNK = 512
+CHUNKS = G * H // CHUNK
+B_TILES = B // P
+ROW_TILES = CHUNK // P
+SCALAR = 0
+VECTOR = 1
+LAST_SPLIT = 384
+
+
+def tile_metalstmcell_pa_kernel(tc, src_x, zx, dx_w, w_x, out_0, out_1):
+    nc = tc.nc
+    src_v = src_x.rearrange("(t p) k -> p t k", p=P)
+    zx_v = zx.rearrange("(t p) g z -> p t (g z)", p=P)
+    dxw_v = dx_w.rearrange("g (t p) z -> p (g t) z", p=P)
+    wx_v = w_x.rearrange("g (t p) k -> p (g t) k", p=P)
+    out0_v = out_0.rearrange("(t p) g h -> p t g h", p=P)
+    out1_v = out_1.rearrange("(t p) g h -> p t g h", p=P)
+
+    with ExitStack() as ctx:
+        const = ctx.enter_context(tc.tile_pool(name="const", bufs=1))
+        raw = ctx.enter_context(tc.tile_pool(name="raw", bufs=1))
+        work = ctx.enter_context(tc.tile_pool(name="work", bufs=2))
+        psum = ctx.enter_context(tc.psum_pool(name="psum", bufs=8))
+
+        zero = const.tile([P, 1], F32, name="zero")
+        scratch = const.tile([P, 1], F32, name="scratch")
+        ident = const.tile([P, P], F32, name="ident")
+        nc.vector.memset(zero[:], 0.0)
+        make_identity(nc, ident[:])
+        nc.scalar.activation(out=scratch[:], in_=zero[:], func=ACT.Identity, bias=zero[:, 0:1], scale=zero[:, 0:1])
+
+        src_rows = []
+        w_rows = []
+        dx_rows = []
+
+        def load_src(j):
+            t = raw.tile([P, 2, IN], BF16, name="src_rows%d" % j)
+            nc.sync.dma_start(out=t[:], in_=src_v[:, 2 * j : 2 * j + 2, :])
+            src_rows.append(t)
+
+        def load_w(n):
+            t = raw.tile([P, 2, IN], BF16, name="w_rows%d" % n)
+            nc.sync.dma_start(out=t[:], in_=wx_v[:, 2 * n : 2 * n + 2, :])
+            w_rows.append(t)
+
+        def load_dx(i):
+            t = raw.tile([P, ROW_TILES, Z], BF16, name="dx_rows%d" % i)
+            nc.sync.dma_start(out=t[:], in_=dxw_v[:, ROW_TILES * i : ROW_TILES * (i + 1), :])
+            dx_rows.append(t)
+
+        load_src(0)
+        load_src(1)
+        load_w(0)
+        load_w(1)
+        zx_first = raw.tile([P, B_TILES, Z], BF16, name="zx_first")
+        nc.sync.dma_start(out=zx_first[:], in_=zx_v[:, :, 0:Z])
+        load_dx(0)
+        load_w(2)
+        load_w(3)
+        load_dx(1)
+        zx_rest = raw.tile([P, B_TILES, (G - 1) * Z], BF16, name="zx_rest")
+        nc.sync.dma_start(out=zx_rest[:], in_=zx_v[:, :, Z : G * Z])
+        for i in range(2, CHUNKS):
+            load_w(2 * i)
+            load_w(2 * i + 1)
+            load_dx(i)
+
+        src_codes = const.tile([P, PASSES, B], U32, name="src_codes", align_bytes=64)
+        src_scales = const.tile([P, PASSES, B], U8, name="src_scales", align_bytes=64)
+        zx_turned = []
+        for g in range(G):
+            t = const.tile([P, B], F32, name="zx_turned%d" % g)
+            zx_turned.append(t)
+        dx_turned = {}
+        w_codes = {}
+        w_scales = {}
+
+        def copy_out(engine, out, in_):
+            if engine == SCALAR:
+                nc.scalar.copy(out=out, in_=in_)
+            else:
+                nc.vector.tensor_copy(out=out, in_=in_)
+
+        def new_grouped():
+            grouped = work.tile([P, PASSES, 4 * CHUNK], BF16, name="grouped", align_bytes=64)
+            return grouped
+
+        def turn_k(rows, grouped, j, engines):
+            for c in range(PASSES):
+                bank = psum.tile([P, 2, 2, P], F32, name="k_bank", tag="bank")
+                for r in range(2):
+                    words = rows[:, r, :].bitcast(F32)
+                    for u in range(2):
+                        nc.tensor.transpose(
+                            out=bank[:, r, u, :],
+                            in_=words[:, WORDS * c + u : WORDS * (c + 1) : 2],
+                            identity=ident[:],
+                        )
+                copy_out(
+                    engines[c],
+                    grouped[:, c, 8 * P * j : 8 * P * (j + 1)].bitcast(F32).rearrange("p (r b u) -> p r b u", r=2, u=2),
+                    bank[:].rearrange("p r u b -> p r b u"),
+                )
+
+        def quantize(grouped, codes, scales):
+            nc.vector.quantize_mx(
+                out=codes[:].rearrange("p c n -> p (c n)").bitcast(FP8X4),
+                scales=scales[:].rearrange("p c n -> p (c n)"),
+                in_=grouped[:].rearrange("p c n -> p (c n)"),
+            )
+
+        def quantize_chunk(i, grouped):
+            w_codes[i] = work.tile([P, PASSES, CHUNK], U32, name="w_codes", align_bytes=64)
+            w_scales[i] = work.tile([P, PASSES, CHUNK], U8, name="w_scales", align_bytes=64)
+            quantize(grouped, w_codes[i], w_scales[i])
+
+        def turn_pairs(tiles, turned):
+            bank = psum.tile([P, 4, P], F32, name="z_bank", tag="bank")
+            for t in range(4):
+                nc.tensor.transpose(out=bank[:, t, :], in_=tiles[t].bitcast(F32), identity=ident[:])
+            nc.scalar.copy(out=turned[:], in_=bank[:].rearrange("p t b -> p (t b)"))
+
+        def turn_dx(i):
+            dx_turned[i] = work.tile([P, CHUNK], F32, name="dx_turned", bufs=3)
+            tiles = []
+            for t in range(ROW_TILES):
+                tiles.append(dx_rows[i][:, t, :])
+            turn_pairs(tiles, dx_turned[i])
+
+        def turn_zx(g):
+            tiles = []
+            for t in range(B_TILES):
+                if g == 0:
+                    tiles.append(zx_first[:, t, :])
+                else:
+                    tiles.append(zx_rest[:, t, Z * (g - 1) : Z * g])
+            turn_pairs(tiles, zx_turned[g])
+
+        def d_x(i, bt):
+            z_pairs = zx_turned[i // 2][:].bitcast(BF16).rearrange("p (b e) -> p b e", e=2)
+            d_pairs = dx_turned[i][:].bitcast(BF16).rearrange("p (h e) -> p h e", e=2)
+            acc = psum.tile([P, CHUNK], F32, name="dx_bank", tag="bank")
+            for e in range(2):
+                nc.tensor.matmul(
+                    out=acc[:],
+                    lhsT=z_pairs[:, P * bt : P * (bt + 1), e],
+                    rhs=d_pairs[:, :, e],
+                    start=(e == 0),
+                    stop=(e == 1),
+                )
+            d_sb = work.tile([P, CHUNK], F32, name="d_sb", bufs=8)
+            nc.scalar.copy(out=d_sb[:], in_=acc[:])
+            return d_sb
+
+        def wx(i, bt):
+            cols = slice(P * bt, P * (bt + 1))
+            acc = psum.tile([P, CHUNK], F32, name="wx_bank", tag="bank")
+            for c in range(PASSES):
+                nc.tensor.matmul_mx(
+                    out=acc[:],
+                    lhsT=src_codes[:, c, cols].bitcast(FP8X4),
+                    lhsT_scale=src_scales[:, c, cols],
+                    rhs=w_codes[i][:, c, :].bitcast(FP8X4),
+                    rhs_scale=w_scales[i][:, c, :],
+                    start=(c == 0),
+                    stop=(c == PASSES - 1),
+                )
+            return acc
+
+        results = {}
+        maxima = {}
+        waiting = []
+        n_cast = [0]
+
+        def multiply(i, bt, acc, d_sb):
+            g, half = i // 2, i % 2
+            cols = slice(CHUNK * half, CHUNK * (half + 1))
+            if half == 0:
+                results[(g, bt)] = work.tile([P, H], F32, name="result", bufs=8)
+            res = results[(g, bt)]
+            nc.vector.tensor_tensor(out=res[:, cols], in0=acc[:], in1=d_sb[:], op=ALU.mult)
+            nc.sync.dma_start(out=out0_v[:, bt, g, cols], in_=res[:, cols])
+
+        def half_max(i, bt):
+            g, half = i // 2, i % 2
+            nc.vector.tensor_reduce(
+                out=maxima[g][:, bt, half : half + 1],
+                in_=results[(g, bt)][:, CHUNK * half : CHUNK * (half + 1)],
+                axis=AX.X,
+                op=ALU.max,
+                apply_absolute_value=True,
+            )
+
+        def factor_steps(g, bts):
+            n = len(bts)
+            amax = work.tile([P, n], F32, name="amax", bufs=3)
+            recip = work.tile([P, n], F32, name="recip", bufs=3)
+            factor = work.tile([P, n], F32, name="factor", bufs=4)
+
+            def combine():
+                nc.vector.tensor_reduce(out=amax[:], in_=maxima[g][:, bts[0] : bts[0] + n, :], axis=AX.X, op=ALU.max)
+
+            def invert():
+                nc.vector.reciprocal(out=recip[:], in_=amax[:])
+
+            def scale():
+                nc.vector.tensor_scalar(out=factor[:], in0=recip[:], scalar1=448.0, scalar2=None, op0=ALU.mult)
+                for n_bt in range(n):
+                    waiting.append((g, bts[n_bt], factor[:, n_bt : n_bt + 1]))
+
+            return [combine, invert, scale]
+
+        def cast_columns(engine, row, codes8, lo, hi):
+            g, bt, factor = row
+            res = results[(g, bt)]
+            if engine == SCALAR:
+                nc.scalar.activation(
+                    out=codes8[:, lo:hi], in_=res[:, lo:hi], func=ACT.Identity, scale=factor, bias=zero[:, 0:1], saturate=False
+                )
+            else:
+                nc.vector.tensor_scalar(
+                    out=codes8[:, lo:hi], in0=res[:, lo:hi], scalar1=factor, scalar2=None, op0=ALU.mult, saturate=False
+                )
+            nc.sync.dma_start(out=out1_v[:, bt, g, lo:hi], in_=codes8[:, lo:hi].bitcast(U8))
+
+        def next_row():
+            row = waiting[n_cast[0]]
+            n_cast[0] += 1
+            codes8 = work.tile([P, H], FP8, name="codes8", bufs=8)
+            return row, codes8
+
+        def cast_next(engine):
+            if n_cast[0] < len(waiting):
+                row, codes8 = next_row()
+                cast_columns(engine, row, codes8, 0, H)
+
+        both = [SCALAR, VECTOR]
+        scalar_only = [SCALAR, SCALAR]
+
+        with tc.manual_schedule():
+            src_grouped = new_grouped()
+            turn_k(src_rows[0], src_grouped, 0, both)
+            turn_k(src_rows[1], src_grouped, 1, both)
+            quantize(src_grouped, src_codes, src_scales)
+            grouped = new_grouped()
+            turn_k(w_rows[0], grouped, 0, scalar_only)
+            turn_k(w_rows[1], grouped, 1, both)
+            quantize_chunk(0, grouped)
+            turn_zx(0)
+            turn_dx(0)
+
+            for i in range(CHUNKS - 1):
+                g, half = i // 2, i % 2
+                if half == 0:
+                    maxima[g] = work.tile([P, B_TILES, 2], F32, name="maxima")
+                grouped = new_grouped()
+                turn_k(w_rows[2 * i + 2], grouped, 0, scalar_only)
+                turn_k(w_rows[2 * i + 3], grouped, 1, scalar_only)
+                d_sb = [d_x(i, 0), d_x(i, 1)]
+                turn_dx(i + 1)
+                if half == 0 and g + 1 < G:
+                    turn_zx(g + 1)
+                d_sb.append(d_x(i, 2))
+                d_sb.append(d_x(i, 3))
+                quantize_chunk(i + 1, grouped)
+                if half == 0:
+                    cast_next(VECTOR)
+                acc = []
+                for bt in range(B_TILES):
+                    acc.append(wx(i, bt))
+                multiply(i, 0, acc[0], d_sb[0])
+                multiply(i, 1, acc[1], d_sb[1])
+                half_max(i, 0)
+                multiply(i, 2, acc[2], d_sb[2])
+                half_max(i, 1)
+                multiply(i, 3, acc[3], d_sb[3])
+                half_max(i, 2)
+                half_max(i, 3)
+                cast_next(SCALAR)
+                if half == 1:
+                    cast_next(SCALAR)
+                    for step in factor_steps(g, [0, 1, 2, 3]):
+                        step()
+
+            i = CHUNKS - 1
+            g = G - 1
+            acc = []
+            d_sb = []
+            for bt in range(B_TILES):
+                d_sb.append(d_x(i, bt))
+                acc.append(wx(i, bt))
+                if bt % 2 == 1:
+                    cast_next(SCALAR)
+            first = factor_steps(g, [0, 1])
+            second = factor_steps(g, [2, 3])
+            multiply(i, 0, acc[0], d_sb[0])
+            multiply(i, 1, acc[1], d_sb[1])
+            half_max(i, 0)
+            multiply(i, 2, acc[2], d_sb[2])
+            half_max(i, 1)
+            multiply(i, 3, acc[3], d_sb[3])
+            first[0]()
+            half_max(i, 2)
+            first[1]()
+            half_max(i, 3)
+            first[2]()
+            second[0]()
+            cast_next(SCALAR)
+            cast_next(VECTOR)
+            second[1]()
+            second[2]()
+            cast_next(VECTOR)
+            row, codes8 = next_row()
+            cast_columns(VECTOR, row, codes8, 0, LAST_SPLIT)
+            cast_columns(SCALAR, row, codes8, LAST_SPLIT, H)

@@ -26,7 +26,9 @@ B_TILES = B // P
 ROW_TILES = CHUNK // P
 SCALAR = 0
 VECTOR = 1
-LAST_SPLIT = 384
+LAST_SPLIT = 352
+SORTED = (5, 7, 9, 11, 13, 15)
+WARM_UP = 6
 
 
 def tile_metalstmcell_pa_kernel(tc, src_x, zx, dx_w, w_x, out_0, out_1):
@@ -48,6 +50,8 @@ def tile_metalstmcell_pa_kernel(tc, src_x, zx, dx_w, w_x, out_0, out_1):
         scratch = const.tile([P, 1], F32, name="scratch")
         ident = const.tile([P, P], F32, name="ident")
         nc.vector.memset(zero[:], 0.0)
+        idle = const.tile([P, CHUNK], BF16, name="idle")
+        nc.vector.memset(idle[:], 0.0)
         make_identity(nc, ident[:])
         nc.scalar.activation(out=scratch[:], in_=zero[:], func=ACT.Identity, bias=zero[:, 0:1], scale=zero[:, 0:1])
 
@@ -106,6 +110,36 @@ def tile_metalstmcell_pa_kernel(tc, src_x, zx, dx_w, w_x, out_0, out_1):
         def new_grouped():
             grouped = work.tile([P, PASSES, 4 * CHUNK], BF16, name="grouped", align_bytes=64)
             return grouped
+
+        w_sorted = {}
+
+        def sort_words(n):
+            t = raw.tile([P, 2, PASSES, 2, P], F32, name="w_sorted%d" % n)
+            for r in range(2):
+                for c in range(PASSES):
+                    nc.gpsimd.tensor_copy(
+                        out=t[:, r, c, :, :],
+                        in_=w_rows[n][:, r, K_PASS * c : K_PASS * (c + 1)].bitcast(F32).rearrange("p (q u) -> p u q", u=2),
+                    )
+            w_sorted[n] = t
+
+        def turn_sorted(n, grouped, j, engines):
+            for c in range(PASSES):
+                bank = psum.tile([P, 2, 2, P], F32, name="k_bank", tag="bank")
+                for r in range(2):
+                    for u in range(2):
+                        nc.tensor.transpose(out=bank[:, r, u, :], in_=w_sorted[n][:, r, c, u, :], identity=ident[:])
+                copy_out(
+                    engines[c],
+                    grouped[:, c, 8 * P * j : 8 * P * (j + 1)].bitcast(F32).rearrange("p (r b u) -> p r b u", r=2, u=2),
+                    bank[:].rearrange("p r u b -> p r b u"),
+                )
+
+        def turn_w(n, grouped, j, engines):
+            if n in SORTED:
+                turn_sorted(n, grouped, j, engines)
+            else:
+                turn_k(w_rows[n], grouped, j, engines)
 
         def turn_k(rows, grouped, j, engines):
             for c in range(PASSES):
@@ -232,6 +266,26 @@ def tile_metalstmcell_pa_kernel(tc, src_x, zx, dx_w, w_x, out_0, out_1):
 
             return [combine, invert, scale]
 
+        def quick_factor(g, bt):
+            q_scale = work.tile([P, 1], F32, name="q_scale", bufs=4)
+            inverse = work.tile([P, 1], F32, name="inverse", bufs=4)
+
+            def combine():
+                nc.vector.tensor_scalar(
+                    out=q_scale[:],
+                    in0=maxima[g][:, bt, 0:1],
+                    scalar1=maxima[g][:, bt, 1:2],
+                    scalar2=1.0 / 448.0,
+                    op0=ALU.max,
+                    op1=ALU.mult,
+                )
+
+            def invert():
+                nc.vector.reciprocal(out=inverse[:], in_=q_scale[:])
+                waiting.append((g, bt, inverse[:, 0:1]))
+
+            return [combine, invert]
+
         def cast_columns(engine, row, codes8, lo, hi):
             g, bt, factor = row
             res = results[(g, bt)]
@@ -260,6 +314,9 @@ def tile_metalstmcell_pa_kernel(tc, src_x, zx, dx_w, w_x, out_0, out_1):
         scalar_only = [SCALAR, SCALAR]
 
         with tc.manual_schedule():
+            idle_bank = psum.tile([P, CHUNK], F32, name="idle_bank", tag="bank")
+            for n in range(WARM_UP):
+                nc.tensor.matmul(out=idle_bank[:], lhsT=idle[:, 0:P], rhs=idle[:], start=True, stop=True)
             src_grouped = new_grouped()
             turn_k(src_rows[0], src_grouped, 0, both)
             turn_k(src_rows[1], src_grouped, 1, both)
@@ -270,14 +327,16 @@ def tile_metalstmcell_pa_kernel(tc, src_x, zx, dx_w, w_x, out_0, out_1):
             quantize_chunk(0, grouped)
             turn_zx(0)
             turn_dx(0)
+            for n in SORTED:
+                sort_words(n)
 
             for i in range(CHUNKS - 1):
                 g, half = i // 2, i % 2
                 if half == 0:
                     maxima[g] = work.tile([P, B_TILES, 2], F32, name="maxima")
                 grouped = new_grouped()
-                turn_k(w_rows[2 * i + 2], grouped, 0, scalar_only)
-                turn_k(w_rows[2 * i + 3], grouped, 1, scalar_only)
+                turn_w(2 * i + 2, grouped, 0, scalar_only)
+                turn_w(2 * i + 3, grouped, 1, scalar_only)
                 d_sb = [d_x(i, 0), d_x(i, 1)]
                 turn_dx(i + 1)
                 if half == 0 and g + 1 < G:
@@ -290,14 +349,10 @@ def tile_metalstmcell_pa_kernel(tc, src_x, zx, dx_w, w_x, out_0, out_1):
                 acc = []
                 for bt in range(B_TILES):
                     acc.append(wx(i, bt))
-                multiply(i, 0, acc[0], d_sb[0])
-                multiply(i, 1, acc[1], d_sb[1])
-                half_max(i, 0)
-                multiply(i, 2, acc[2], d_sb[2])
-                half_max(i, 1)
-                multiply(i, 3, acc[3], d_sb[3])
-                half_max(i, 2)
-                half_max(i, 3)
+                for bt in range(B_TILES):
+                    multiply(i, bt, acc[bt], d_sb[bt])
+                for bt in range(B_TILES):
+                    half_max(i, bt)
                 cast_next(SCALAR)
                 if half == 1:
                     cast_next(SCALAR)
@@ -313,25 +368,28 @@ def tile_metalstmcell_pa_kernel(tc, src_x, zx, dx_w, w_x, out_0, out_1):
                 acc.append(wx(i, bt))
                 if bt % 2 == 1:
                     cast_next(SCALAR)
-            first = factor_steps(g, [0, 1])
-            second = factor_steps(g, [2, 3])
+            chain = []
+            for bt in range(B_TILES):
+                chain.append(quick_factor(g, bt))
             multiply(i, 0, acc[0], d_sb[0])
             multiply(i, 1, acc[1], d_sb[1])
             half_max(i, 0)
             multiply(i, 2, acc[2], d_sb[2])
+            chain[0][0]()
             half_max(i, 1)
-            multiply(i, 3, acc[3], d_sb[3])
-            first[0]()
-            half_max(i, 2)
-            first[1]()
-            half_max(i, 3)
-            first[2]()
-            second[0]()
+            chain[0][1]()
             cast_next(SCALAR)
-            cast_next(VECTOR)
-            second[1]()
-            second[2]()
-            cast_next(VECTOR)
+            multiply(i, 3, acc[3], d_sb[3])
+            chain[1][0]()
+            half_max(i, 2)
+            chain[1][1]()
+            cast_next(SCALAR)
+            half_max(i, 3)
+            chain[2][0]()
+            chain[3][0]()
+            chain[2][1]()
+            chain[3][1]()
             row, codes8 = next_row()
-            cast_columns(VECTOR, row, codes8, 0, LAST_SPLIT)
             cast_columns(SCALAR, row, codes8, LAST_SPLIT, H)
+            cast_columns(VECTOR, row, codes8, 0, LAST_SPLIT)
+            cast_next(VECTOR)

@@ -28,7 +28,7 @@ SCALAR = 0
 VECTOR = 1
 LAST_SPLIT = 352
 SORTED = (5, 7, 9, 11, 13, 15)
-WARM_UP = 6
+WARM_UP = 4
 
 
 def tile_metalstmcell_pa_kernel(tc, src_x, zx, dx_w, w_x, out_0, out_1):
@@ -74,22 +74,23 @@ def tile_metalstmcell_pa_kernel(tc, src_x, zx, dx_w, w_x, out_0, out_1):
             nc.sync.dma_start(out=t[:], in_=dxw_v[:, ROW_TILES * i : ROW_TILES * (i + 1), :])
             dx_rows.append(t)
 
+        zx_first = raw.tile([P, B_TILES, Z], BF16, name="zx_first")
+        nc.sync.dma_start(out=zx_first[:], in_=zx_v[:, :, 0:Z])
+        load_dx(0)
         load_src(0)
         load_src(1)
         load_w(0)
         load_w(1)
-        zx_first = raw.tile([P, B_TILES, Z], BF16, name="zx_first")
-        nc.sync.dma_start(out=zx_first[:], in_=zx_v[:, :, 0:Z])
-        load_dx(0)
         load_w(2)
         load_w(3)
         load_dx(1)
         zx_rest = raw.tile([P, B_TILES, (G - 1) * Z], BF16, name="zx_rest")
-        nc.sync.dma_start(out=zx_rest[:], in_=zx_v[:, :, Z : G * Z])
         for i in range(2, CHUNKS):
             load_w(2 * i)
             load_w(2 * i + 1)
             load_dx(i)
+            if i == 2:
+                nc.sync.dma_start(out=zx_rest[:], in_=zx_v[:, :, Z : G * Z])
 
         src_codes = const.tile([P, PASSES, B], U32, name="src_codes", align_bytes=64)
         src_scales = const.tile([P, PASSES, B], U8, name="src_scales", align_bytes=64)
@@ -317,16 +318,20 @@ def tile_metalstmcell_pa_kernel(tc, src_x, zx, dx_w, w_x, out_0, out_1):
             idle_bank = psum.tile([P, CHUNK], F32, name="idle_bank", tag="bank")
             for n in range(WARM_UP):
                 nc.tensor.matmul(out=idle_bank[:], lhsT=idle[:, 0:P], rhs=idle[:], start=True, stop=True)
-            src_grouped = new_grouped()
-            turn_k(src_rows[0], src_grouped, 0, both)
-            turn_k(src_rows[1], src_grouped, 1, both)
-            quantize(src_grouped, src_codes, src_scales)
-            grouped = new_grouped()
-            turn_k(w_rows[0], grouped, 0, scalar_only)
-            turn_k(w_rows[1], grouped, 1, both)
-            quantize_chunk(0, grouped)
             turn_zx(0)
             turn_dx(0)
+            src_grouped = new_grouped()
+            turn_k(src_rows[0], src_grouped, 0, both)
+            first_d = [d_x(0, 0)]
+            turn_k(src_rows[1], src_grouped, 1, both)
+            quantize(src_grouped, src_codes, src_scales)
+            first_d.append(d_x(0, 1))
+            grouped = new_grouped()
+            turn_k(w_rows[0], grouped, 0, scalar_only)
+            first_d.append(d_x(0, 2))
+            turn_k(w_rows[1], grouped, 1, both)
+            quantize_chunk(0, grouped)
+            first_d.append(d_x(0, 3))
             for n in SORTED:
                 sort_words(n)
 
@@ -337,12 +342,16 @@ def tile_metalstmcell_pa_kernel(tc, src_x, zx, dx_w, w_x, out_0, out_1):
                 grouped = new_grouped()
                 turn_w(2 * i + 2, grouped, 0, scalar_only)
                 turn_w(2 * i + 3, grouped, 1, scalar_only)
-                d_sb = [d_x(i, 0), d_x(i, 1)]
+                if i == 0:
+                    d_sb = first_d
+                else:
+                    d_sb = [d_x(i, 0), d_x(i, 1)]
                 turn_dx(i + 1)
-                if half == 0 and g + 1 < G:
+                if half == 1 and g + 1 < G:
                     turn_zx(g + 1)
-                d_sb.append(d_x(i, 2))
-                d_sb.append(d_x(i, 3))
+                if i > 0:
+                    d_sb.append(d_x(i, 2))
+                    d_sb.append(d_x(i, 3))
                 quantize_chunk(i + 1, grouped)
                 if half == 0:
                     cast_next(VECTOR)

@@ -340,12 +340,15 @@ def tile_metalstmcell_pa_kernel(tc, src_x, zx, dx_w, w_x, out_0, out_1):
                 if half == 0:
                     maxima[g] = work.tile([P, B_TILES, 2], F32, name="maxima")
                 grouped = new_grouped()
-                turn_w(2 * i + 2, grouped, 0, scalar_only)
-                turn_w(2 * i + 3, grouped, 1, scalar_only)
                 if i == 0:
+                    turn_w(2 * i + 2, grouped, 0, scalar_only)
+                    turn_w(2 * i + 3, grouped, 1, scalar_only)
                     d_sb = first_d
                 else:
-                    d_sb = [d_x(i, 0), d_x(i, 1)]
+                    turn_w(2 * i + 2, grouped, 0, scalar_only)
+                    d_sb = [d_x(i, 0)]
+                    turn_w(2 * i + 3, grouped, 1, scalar_only)
+                    d_sb.append(d_x(i, 1))
                 turn_dx(i + 1)
                 if half == 1 and g + 1 < G:
                     turn_zx(g + 1)

from contextlib import ExitStack

import concourse.mybir as mybir
from concourse.masks import make_identity

B, IN, H, Z, G = 512, 1024, 1024, 256, 4
FLOPS = 2 * B * G * H * IN + 2 * B * G * H * Z

F32 = mybir.dt.float32
BF16 = mybir.dt.bfloat16
U32 = mybir.dt.uint32
U8 = mybir.dt.uint8
FP8X4 = mybir.dt.float8_e4m3fn_x4
FP8 = mybir.dt.float8_e4m3fn
ALU = mybir.AluOpType
ACT = mybir.ActivationFunctionType
AX = mybir.AxisListType

P = 128
K_PASS = 4 * P
PASSES = IN // K_PASS
WORDS = K_PASS // 2
CHUNK = 512
CHUNKS = G * H // CHUNK
B_TILES = B // P
ROW_TILES = CHUNK // P
SCALAR = 0
VECTOR = 1
LAST_SPLIT = 352
SORTED = (5, 7, 9, 11, 13, 15)
WARM_UP = 4


def tile_metalstmcell_pa_kernel(tc, src_x, zx, dx_w, w_x, out_0, out_1):
    nc = tc.nc
    src_v = src_x.rearrange("(t p) k -> p t k", p=P)
    zx_v = zx.rearrange("(t p) g z -> p t (g z)", p=P)
    dxw_v = dx_w.rearrange("g (t p) z -> p (g t) z", p=P)
    wx_v = w_x.rearrange("g (t p) k -> p (g t) k", p=P)
    out0_v = out_0.rearrange("(t p) g h -> p t g h", p=P)
    out1_v = out_1.rearrange("(t p) g h -> p t g h", p=P)

    with ExitStack() as ctx:
        const = ctx.enter_context(tc.tile_pool(name="const", bufs=1))
        raw = ctx.enter_context(tc.tile_pool(name="raw", bufs=1))
        work = ctx.enter_context(tc.tile_pool(name="work", bufs=2))
        psum = ctx.enter_context(tc.psum_pool(name="psum", bufs=8))

        zero = const.tile([P, 1], F32, name="zero")
        scratch = const.tile([P, 1], F32, name="scratch")
        ident = const.tile([P, P], F32, name="ident")
        nc.vector.memset(zero[:], 0.0)
        idle = const.tile([P, CHUNK], BF16, name="idle")
        nc.vector.memset(idle[:], 0.0)
        make_identity(nc, ident[:])
        nc.scalar.activation(out=scratch[:], in_=zero[:], func=ACT.Identity, bias=zero[:, 0:1], scale=zero[:, 0:1])

        src_rows = []
        w_rows = []
        dx_rows = []

        def load_src(j):
            t = raw.tile([P, 2, IN], BF16, name="src_rows%d" % j)
            nc.sync.dma_start(out=t[:], in_=src_v[:, 2 * j : 2 * j + 2, :])
            src_rows.append(t)

        def load_w(n):
            t = raw.tile([P, 2, IN], BF16, name="w_rows%d" % n)
            nc.sync.dma_start(out=t[:], in_=wx_v[:, 2 * n : 2 * n + 2, :])
            w_rows.append(t)

        def load_dx(i):
            t = raw.tile([P, ROW_TILES, Z], BF16, name="dx_rows%d" % i)
            nc.sync.dma_start(out=t[:], in_=dxw_v[:, ROW_TILES * i : ROW_TILES * (i + 1), :])
            dx_rows.append(t)

        zx_first = raw.tile([P, B_TILES, Z], BF16, name="zx_first")
        nc.sync.dma_start(out=zx_first[:], in_=zx_v[:, :, 0:Z])
        load_dx(0)
        load_src(0)
        load_src(1)
        load_w(0)
        load_w(1)
        load_w(2)
        load_w(3)
        load_dx(1)
        zx_rest = raw.tile([P, B_TILES, (G - 1) * Z], BF16, name="zx_rest")
        for i in range(2, CHUNKS):
            load_w(2 * i)
            load_w(2 * i + 1)
            load_dx(i)
            if i == 2:
                nc.sync.dma_start(out=zx_rest[:], in_=zx_v[:, :, Z : G * Z])

        src_codes = const.tile([P, PASSES, B], U32, name="src_codes", align_bytes=64)
        src_scales = const.tile([P, PASSES, B], U8, name="src_scales", align_bytes=64)
        zx_turned = []
        for g in range(G):
            t = const.tile([P, B], F32, name="zx_turned%d" % g)
            zx_turned.append(t)
        dx_turned = {}
        w_codes = {}
        w_scales = {}

        def copy_out(engine, out, in_):
            if engine == SCALAR:
                nc.scalar.copy(out=out, in_=in_)
            else:
                nc.vector.tensor_copy(out=out, in_=in_)

        def new_grouped():
            grouped = work.tile([P, PASSES, 4 * CHUNK], BF16, name="grouped", align_bytes=64)
            return grouped

        w_sorted = {}

        def sort_words(n):
            t = raw.tile([P, 2, PASSES, 2, P], F32, name="w_sorted%d" % n)
            for r in range(2):
                for c in range(PASSES):
                    nc.gpsimd.tensor_copy(
                        out=t[:, r, c, :, :],
                        in_=w_rows[n][:, r, K_PASS * c : K_PASS * (c + 1)].bitcast(F32).rearrange("p (q u) -> p u q", u=2),
                    )
            w_sorted[n] = t

        def turn_sorted(n, grouped, j, engines):
            for c in range(PASSES):
                bank = psum.tile([P, 2, 2, P], F32, name="k_bank", tag="bank")
                for r in range(2):
                    for u in range(2):
                        nc.tensor.transpose(out=bank[:, r, u, :], in_=w_sorted[n][:, r, c, u, :], identity=ident[:])
                copy_out(
                    engines[c],
                    grouped[:, c, 8 * P * j : 8 * P * (j + 1)].bitcast(F32).rearrange("p (r b u) -> p r b u", r=2, u=2),
                    bank[:].rearrange("p r u b -> p r b u"),
                )

        def turn_w(n, grouped, j, engines):
            if n in SORTED:
                turn_sorted(n, grouped, j, engines)
            else:
                turn_k(w_rows[n], grouped, j, engines)

        def turn_k(rows, grouped, j, engines):
            for c in range(PASSES):
                bank = psum.tile([P, 2, 2, P], F32, name="k_bank", tag="bank")
                for r in range(2):
                    words = rows[:, r, :].bitcast(F32)
                    for u in range(2):
                        nc.tensor.transpose(
                            out=bank[:, r, u, :],
                            in_=words[:, WORDS * c + u : WORDS * (c + 1) : 2],
                            identity=ident[:],
                        )
                copy_out(
                    engines[c],
                    grouped[:, c, 8 * P * j : 8 * P * (j + 1)].bitcast(F32).rearrange("p (r b u) -> p r b u", r=2, u=2),
                    bank[:].rearrange("p r u b -> p r b u"),
                )

        def quantize(grouped, codes, scales):
            nc.vector.quantize_mx(
                out=codes[:].rearrange("p c n -> p (c n)").bitcast(FP8X4),
                scales=scales[:].rearrange("p c n -> p (c n)"),
                in_=grouped[:].rearrange("p c n -> p (c n)"),
            )

        def quantize_chunk(i, grouped):
            w_codes[i] = work.tile([P, PASSES, CHUNK], U32, name="w_codes", align_bytes=64)
            w_scales[i] = work.tile([P, PASSES, CHUNK], U8, name="w_scales", align_bytes=64)
            quantize(grouped, w_codes[i], w_scales[i])

        def turn_pairs(tiles, turned):
            bank = psum.tile([P, 4, P], F32, name="z_bank", tag="bank")
            for t in range(4):
                nc.tensor.transpose(out=bank[:, t, :], in_=tiles[t].bitcast(F32), identity=ident[:])
            nc.scalar.copy(out=turned[:], in_=bank[:].rearrange("p t b -> p (t b)"))

        def turn_dx(i):
            dx_turned[i] = work.tile([P, CHUNK], F32, name="dx_turned", bufs=3)
            tiles = []
            for t in range(ROW_TILES):
                tiles.append(dx_rows[i][:, t, :])
            turn_pairs(tiles, dx_turned[i])

        def turn_zx(g):
            tiles = []
            for t in range(B_TILES):
                if g == 0:
                    tiles.append(zx_first[:, t, :])
                else:
                    tiles.append(zx_rest[:, t, Z * (g - 1) : Z * g])
            turn_pairs(tiles, zx_turned[g])

        def d_x(i, bt):
            z_pairs = zx_turned[i // 2][:].bitcast(BF16).rearrange("p (b e) -> p b e", e=2)
            d_pairs = dx_turned[i][:].bitcast(BF16).rearrange("p (h e) -> p h e", e=2)
            acc = psum.tile([P, CHUNK], F32, name="dx_bank", tag="bank")
            for e in range(2):
                nc.tensor.matmul(
                    out=acc[:],
                    lhsT=z_pairs[:, P * bt : P * (bt + 1), e],
                    rhs=d_pairs[:, :, e],
                    start=(e == 0),
                    stop=(e == 1),
                )
            d_sb = work.tile([P, CHUNK], F32, name="d_sb", bufs=8)
            nc.scalar.copy(out=d_sb[:], in_=acc[:])
            return d_sb

        def wx(i, bt):
            cols = slice(P * bt, P * (bt + 1))
            acc = psum.tile([P, CHUNK], F32, name="wx_bank", tag="bank")
            for c in range(PASSES):
                nc.tensor.matmul_mx(
                    out=acc[:],
                    lhsT=src_codes[:, c, cols].bitcast(FP8X4),
                    lhsT_scale=src_scales[:, c, cols],
                    rhs=w_codes[i][:, c, :].bitcast(FP8X4),
                    rhs_scale=w_scales[i][:, c, :],
                    start=(c == 0),
                    stop=(c == PASSES - 1),
                )
            return acc

        results = {}
        maxima = {}
        waiting = []
        n_cast = [0]

        def multiply(i, bt, acc, d_sb):
            g, half = i // 2, i % 2
            cols = slice(CHUNK * half, CHUNK * (half + 1))
            if half == 0:
                results[(g, bt)] = work.tile([P, H], F32, name="result", bufs=8)
            res = results[(g, bt)]
            nc.vector.tensor_tensor(out=res[:, cols], in0=acc[:], in1=d_sb[:], op=ALU.mult)
            nc.sync.dma_start(out=out0_v[:, bt, g, cols], in_=res[:, cols])

        def half_max(i, bt):
            g, half = i // 2, i % 2
            nc.vector.tensor_reduce(
                out=maxima[g][:, bt, half : half + 1],
                in_=results[(g, bt)][:, CHUNK * half : CHUNK * (half + 1)],
                axis=AX.X,
                op=ALU.max,
                apply_absolute_value=True,
            )

        def factor_steps(g, bts):
            n = len(bts)
            amax = work.tile([P, n], F32, name="amax", bufs=3)
            recip = work.tile([P, n], F32, name="recip", bufs=3)
            factor = work.tile([P, n], F32, name="factor", bufs=4)

            def combine():
                nc.vector.tensor_reduce(out=amax[:], in_=maxima[g][:, bts[0] : bts[0] + n, :], axis=AX.X, op=ALU.max)

            def invert():
                nc.vector.reciprocal(out=recip[:], in_=amax[:])

            def scale():
                nc.vector.tensor_scalar(out=factor[:], in0=recip[:], scalar1=448.0, scalar2=None, op0=ALU.mult)
                for n_bt in range(n):
                    waiting.append((g, bts[n_bt], factor[:, n_bt : n_bt + 1]))

            return [combine, invert, scale]

        def quick_factor(g, bt):
            q_scale = work.tile([P, 1], F32, name="q_scale", bufs=4)
            inverse = work.tile([P, 1], F32, name="inverse", bufs=4)

            def combine():
                nc.vector.tensor_scalar(
                    out=q_scale[:],
                    in0=maxima[g][:, bt, 0:1],
                    scalar1=maxima[g][:, bt, 1:2],
                    scalar2=1.0 / 448.0,
                    op0=ALU.max,
                    op1=ALU.mult,
                )

            def invert():
                nc.vector.reciprocal(out=inverse[:], in_=q_scale[:])
                waiting.append((g, bt, inverse[:, 0:1]))

            return [combine, invert]

        def cast_columns(engine, row, codes8, lo, hi):
            g, bt, factor = row
            res = results[(g, bt)]
            if engine == SCALAR:
                nc.scalar.activation(
                    out=codes8[:, lo:hi], in_=res[:, lo:hi], func=ACT.Identity, scale=factor, bias=zero[:, 0:1], saturate=False
                )
            else:
                nc.vector.tensor_scalar(
                    out=codes8[:, lo:hi], in0=res[:, lo:hi], scalar1=factor, scalar2=None, op0=ALU.mult, saturate=False
                )
            nc.sync.dma_start(out=out1_v[:, bt, g, lo:hi], in_=codes8[:, lo:hi].bitcast(U8))

        def next_row():
            row = waiting[n_cast[0]]
            n_cast[0] += 1
            codes8 = work.tile([P, H], FP8, name="codes8", bufs=8)
            return row, codes8

        def cast_next(engine):
            if n_cast[0] < len(waiting):
                row, codes8 = next_row()
                cast_columns(engine, row, codes8, 0, H)

        both = [SCALAR, VECTOR]
        scalar_only = [SCALAR, SCALAR]

        with tc.manual_schedule():
            idle_bank = psum.tile([P, CHUNK], F32, name="idle_bank", tag="bank")
            for n in range(WARM_UP):
                nc.tensor.matmul(out=idle_bank[:], lhsT=idle[:, 0:P], rhs=idle[:], start=True, stop=True)
            turn_zx(0)
            turn_dx(0)
            src_grouped = new_grouped()
            turn_k(src_rows[0], src_grouped, 0, both)
            first_d = [d_x(0, 0)]
            turn_k(src_rows[1], src_grouped, 1, both)
            quantize(src_grouped, src_codes, src_scales)
            first_d.append(d_x(0, 1))
            grouped = new_grouped()
            turn_k(w_rows[0], grouped, 0, scalar_only)
            first_d.append(d_x(0, 2))
            turn_k(w_rows[1], grouped, 1, both)
            quantize_chunk(0, grouped)
            first_d.append(d_x(0, 3))
            for n in SORTED:
                sort_words(n)

            for i in range(CHUNKS - 1):
                g, half = i // 2, i % 2
                if half == 0:
                    maxima[g] = work.tile([P, B_TILES, 2], F32, name="maxima")
                grouped = new_grouped()
                if i == 0:
                    turn_w(2 * i + 2, grouped, 0, scalar_only)
                    turn_w(2 * i + 3, grouped, 1, scalar_only)
                    d_sb = first_d
                else:
                    turn_w(2 * i + 2, grouped, 0, scalar_only)
                    d_sb = [d_x(i, 0)]
                    turn_w(2 * i + 3, grouped, 1, scalar_only)
                    d_sb.append(d_x(i, 1))
                turn_dx(i + 1)
                if half == 1 and g + 1 < G:
                    turn_zx(g + 1)
                if i > 0:
                    d_sb.append(d_x(i, 2))
                    d_sb.append(d_x(i, 3))
                quantize_chunk(i + 1, grouped)
                if half == 0:
                    cast_next(VECTOR)
                acc = []
                for bt in range(B_TILES):
                    acc.append(wx(i, bt))
                for bt in range(B_TILES):
                    multiply(i, bt, acc[bt], d_sb[bt])
                for bt in range(B_TILES):
                    half_max(i, bt)
                cast_next(SCALAR)
                if half == 1:
                    cast_next(SCALAR)
                    for step in factor_steps(g, [0, 1, 2, 3]):
                        step()

            i = CHUNKS - 1
            g = G - 1
            acc = []
            d_sb = []
            for bt in range(B_TILES):
                d_sb.append(d_x(i, bt))
                acc.append(wx(i, bt))
                if bt % 2 == 1:
                    cast_next(SCALAR)
            chain = []
            for bt in range(B_TILES):
                chain.append(quick_factor(g, bt))
            multiply(i, 0, acc[0], d_sb[0])
            multiply(i, 1, acc[1], d_sb[1])
            half_max(i, 0)
            multiply(i, 2, acc[2], d_sb[2])
            chain[0][0]()
            half_max(i, 1)
            chain[0][1]()
            cast_next(SCALAR)
            multiply(i, 3, acc[3], d_sb[3])
            chain[1][0]()
            half_max(i, 2)
            chain[1][1]()
            cast_next(SCALAR)
            half_max(i, 3)
            chain[2][0]()
            chain[3][0]()
            chain[2][1]()
            chain[3][1]()
            row, codes8 = next_row()
            cast_columns(SCALAR, row, codes8, LAST_SPLIT, H)
            cast_columns(VECTOR, row, codes8, 0, LAST_SPLIT)
            cast_next(VECTOR)
